import numpy as np
import ml_dtypes


def mxq(x, axis, fmt="e4m3"):
    dtype, down = {"e4m3": (ml_dtypes.float8_e4m3fn, 7), "e5m2": (ml_dtypes.float8_e5m2, 14)}[fmt]
    v = np.moveaxis(np.asarray(x, np.float32).astype(ml_dtypes.bfloat16).astype(np.float64), axis, -1)
    blocks = v.reshape(v.shape[:-1] + (-1, 32))
    amax = np.abs(blocks).max(-1, keepdims=True)
    byte = np.maximum(np.where(amax > 0, np.frexp(amax)[1] - 1 + 127, 0) - down, 1)
    scale = np.exp2(byte - 127.0)
    codes = (blocks / scale).astype(np.float32).astype(dtype).astype(np.float64)
    return np.moveaxis((codes * scale).reshape(v.shape), -1, axis)


WIDE = False


def mx_kscale(k):
    if not WIDE:
        return np.ones(k)
    levels = np.array([30, -30])
    if k % 512:
        return np.exp2(np.random.permutation(np.resize(levels, k // 32))).repeat(32)
    a = np.empty((k // 512, 16))
    for p in range(k // 512):
        a[p, :8] = np.random.permutation(np.resize(levels, 8))
        for g in range(8):
            far = levels[np.abs(levels - a[p, g]) >= 10]
            a[p, g + 8] = far[np.random.randint(len(far))]
    return np.exp2(a.ravel()).repeat(32)


BF16 = ml_dtypes.bfloat16


def bf(x):
    return np.asarray(x, np.float32).astype(BF16)


def f64(x):
    return np.asarray(x).astype(np.float64)


B, S, M, H, KV, HD = 2, 256, 2048, 16, 4, 128
ROT = HD // 4
HALF = ROT // 2
EPS = 1e-6
MAX_WAVELENGTH = 10000.0


def rms_norm(x, scale):
    var = np.mean(np.square(x), axis=-1, keepdims=True)
    return x * (1.0 / np.sqrt(var + EPS)) * scale


def partial_rope(x):
    x_rope, x_pass = x[..., :ROT], x[..., ROT:]
    pos = np.arange(S, dtype=np.float64)
    inv_freq = 1.0 / (MAX_WAVELENGTH ** (np.arange(0, ROT, 2, dtype=np.float64) / ROT))
    freq = pos[:, None] * inv_freq[None, :]
    emb = np.concatenate([freq, freq], axis=-1)
    cos = np.cos(emb)[None, :, None, :]
    sin = np.sin(emb)[None, :, None, :]
    x1, x2 = x_rope[..., :HALF], x_rope[..., HALF:]
    rotated = np.concatenate([-x2, x1], axis=-1)
    x_rope = x_rope * cos + rotated * sin
    return np.concatenate([x_rope, x_pass], axis=-1)


def setup_inputs():
    s = mx_kscale(M)
    w = 1.0 / np.sqrt(M) / s[:, None, None]
    return {"hidden_states": bf(np.random.standard_normal((B, S, M)) * s),
            "Wq_query": bf(np.random.standard_normal((M, H, HD)) * w),
            "Wk": bf(np.random.standard_normal((M, KV, HD)) * w),
            "Wv": bf(np.random.standard_normal((M, KV, HD)) * 2.0 * w),
            "q_scale": bf(1.0 + 0.1 * np.random.standard_normal(HD)),
            "k_scale": bf(1.0 + 0.1 * np.random.standard_normal(HD))}


def reference(hidden_states, Wq_query, Wk, Wv, q_scale, k_scale):
    xq = mxq(f64(hidden_states).reshape(B * S, M), 1, "e5m2")
    query = (xq @ mxq(f64(Wq_query).reshape(M, H * HD), 0, "e5m2")).reshape(B, S, H, HD)
    key = (xq @ mxq(f64(Wk).reshape(M, KV * HD), 0, "e5m2")).reshape(B, S, KV, HD)
    value = (xq @ mxq(f64(Wv).reshape(M, KV * HD), 0, "e5m2")).reshape(B, S, KV, HD)
    query = partial_rope(rms_norm(query, f64(q_scale)))
    key = partial_rope(rms_norm(key, f64(k_scale)))
    return query, key, value

@@ -1,0 +1,310 @@
+import math
+from contextlib import ExitStack
+
+import concourse.mybir as mybir
+from concourse.masks import make_identity
+
+B, S, M, H, KV, HD = 2, 256, 2048, 16, 4, 128
+ROT = HD // 4
+HALF = ROT // 2
+EPS = 1e-6
+MAX_WAVELENGTH = 10000.0
+FLOPS = 2 * B * S * M * (H + 2 * KV) * HD
+
+F32 = mybir.dt.float32
+BF16 = mybir.dt.bfloat16
+I32 = mybir.dt.int32
+U32 = mybir.dt.uint32
+U8 = mybir.dt.uint8
+E5M2X4 = mybir.dt.float8_e5m2_x4
+ALU = mybir.AluOpType
+ACT = mybir.ActivationFunctionType
+
+P = 128
+PACK = 4
+K_PASS = P * PACK
+PASSES = M // K_PASS
+TOKEN_TILES = B * S // P
+POS_TILES = S // P
+COLS = 512
+HEADS = COLS // HD
+COL_TILES = (H + 2 * KV) // HEADS
+CHUNKS = COL_TILES * PASSES
+NORMED_BANKS = (COL_TILES - 1) * TOKEN_TILES
+V_COLS_HEAD = 328
+V_COLS = 216
+
+
+def tile_qwen3_5attention_pa_kernel(
+    tc, hidden_states, Wq_query, Wk, Wv, q_scale, k_scale, out_0, out_1, out_2
+):
+    nc = tc.nc
+    x_hbm = hidden_states.rearrange("b s m -> (b s) m")
+    wq = Wq_query.rearrange("m h d -> m (h d)")
+    wk = Wk.rearrange("m h d -> m (h d)")
+    wv = Wv.rearrange("m h d -> m (h d)")
+    q_out = out_0.rearrange("b s h d -> (b s) (h d)")
+    k_out = out_1.rearrange("b s h d -> (b s) (h d)")
+    v_out = out_2.rearrange("b s h d -> (b s) (h d)")
+    outs = [k_out] + [q_out[:, c : c + COLS] for c in range(0, H * HD, COLS)] + [v_out]
+    gain_of_tile = [1, 0, 0, 0, 0]
+
+    with ExitStack() as ctx:
+        keep = ctx.enter_context(tc.tile_pool(name="keep", bufs=1))
+        work = ctx.enter_context(tc.tile_pool(name="work", bufs=3))
+        psum = ctx.enter_context(tc.psum_pool(name="psum", bufs=1))
+        ctx.enter_context(tc.manual_schedule())
+
+        def bank(index):
+            return psum.tile([P, COLS], F32, name="bank%d" % index)
+
+        gain_rows = keep.tile([P, 2 * HD], BF16)
+        nc.gpsimd.memset(gain_rows[:], 0.0)
+        position = keep.tile([P, POS_TILES], I32)
+        nc.gpsimd.iota(position[:], pattern=[[P, POS_TILES]], base=0, channel_multiplier=1)
+        ones = keep.tile([P, P], BF16)
+        nc.gpsimd.memset(ones[:], 1.0)
+        ident = keep.tile([P, P], F32)
+        make_identity(nc, ident[:])
+
+        nc.scalar.dma_start(out=gain_rows[0:1, 0:HD], in_=q_scale.rearrange("(o d) -> o d", o=1))
+        nc.scalar.dma_start(out=gain_rows[0:1, HD : 2 * HD], in_=k_scale.rearrange("(o d) -> o d", o=1))
+
+        w_raw = []
+        x_raw = []
+
+        def load_w(w, col0, width, g):
+            raw = keep.tile([P, PACK, width], BF16, name="w_raw%d" % len(w_raw), align_bytes=64)
+            rows = w[g * K_PASS : (g + 1) * K_PASS, col0 : col0 + width]
+            nc.sync.dma_start(out=raw[:], in_=rows.rearrange("(p t) n -> p t n", t=PACK))
+            return raw
+
+        for g in range(PASSES):
+            w_raw.append(load_w(wk, 0, COLS, g)[:])
+            xt = keep.tile([P, M], BF16, name="x_raw%d" % g, align_bytes=64)
+            nc.sync.dma_start(out=xt[:], in_=x_hbm[g * P : (g + 1) * P, :])
+            x_raw.append(xt)
+        for col0 in (0, COLS):
+            for g in range(PASSES):
+                w_raw.append(load_w(wq, col0, COLS, g)[:])
+        wide = []
+        for g in range(PASSES):
+            raw = load_w(wq, 2 * COLS, 2 * COLS, g)
+            wide.append(raw)
+            w_raw.append(raw[:, :, 0:COLS])
+        for g in range(PASSES):
+            w_raw.append(wide[g][:, :, COLS : 2 * COLS])
+        for g in range(PASSES):
+            w_raw.append(load_w(wv, 0, COLS, g)[:])
+
+        turns = keep.tile([P, 2, POS_TILES, HALF], F32)
+        for i in range(HALF):
+            per_position = MAX_WAVELENGTH ** (-i / HALF) / (2.0 * math.pi)
+            nc.vector.tensor_scalar(turns[:, 1, :, i], position[:], per_position, None, ALU.mult)
+        nc.vector.tensor_scalar(turns[:, 0, :, :], turns[:, 1, :, :], 0.25, None, ALU.add)
+        flat_turns = turns[:].rearrange("p f h i -> p (f h i)")
+        whole = keep.tile([P, 2 * POS_TILES * HALF], I32)
+        nc.vector.tensor_copy(whole[:], flat_turns)
+        frac = keep.tile([P, 2 * POS_TILES * HALF], F32)
+        nc.vector.tensor_tensor(frac[:], flat_turns, whole[:], ALU.subtract)
+        neg_frac = keep.tile([P, 2 * POS_TILES * HALF], F32)
+        nc.vector.scalar_tensor_tensor(neg_frac[:], frac[:], 0.5, frac[:], ALU.is_gt, ALU.subtract)
+        trig = keep.tile([P, 2, 1, POS_TILES, HALF], F32)
+        nc.scalar.activation(
+            trig[:].rearrange("p f o h i -> p (f o h i)"), neg_frac[:], ACT.Sin, scale=-2.0 * math.pi
+        )
+
+        direct = keep.tile([P, 2, POS_TILES, HD], F32)
+        cross = keep.tile([P, 2, POS_TILES, ROT], F32)
+
+        def build_tables(gains):
+            g4 = gains[:, 0 : 2 * HD].rearrange("p (w o d) -> p w o d", w=2, o=1)
+            shape = [P, 2, POS_TILES, HALF]
+            cos = trig[:, 0, :, :, :].to_broadcast(shape)
+            sin = trig[:, 1, :, :, :].to_broadcast(shape)
+            neg_sin = keep.tile([P, 1, POS_TILES, HALF], F32)
+            nc.vector.tensor_scalar(neg_sin[:], trig[:, 1, :, :, :], -1.0, None, ALU.mult)
+            lo = g4[:, :, :, 0:HALF].to_broadcast(shape)
+            hi = g4[:, :, :, HALF:ROT].to_broadcast(shape)
+            nc.vector.tensor_tensor(direct[:, :, :, 0:HALF], lo, cos, ALU.mult)
+            nc.vector.tensor_tensor(direct[:, :, :, HALF:ROT], hi, cos, ALU.mult)
+            nc.vector.tensor_copy(
+                direct[:, :, :, ROT:HD], g4[:, :, :, ROT:HD].to_broadcast([P, 2, POS_TILES, HD - ROT])
+            )
+            nc.vector.tensor_tensor(cross[:, :, :, 0:HALF], lo, sin, ALU.mult)
+            nc.vector.tensor_tensor(cross[:, :, :, HALF:ROT], hi, neg_sin[:].to_broadcast(shape), ALU.mult)
+
+        grouped = {}
+        w_codes = {}
+        w_scales = {}
+        x_banks = {}
+        x_grouped = {}
+        x_codes = {}
+        x_scales = {}
+        acc = {}
+        sum_sq = {}
+        inv_rms = {}
+
+        def interleave(engine_copy, c, col0, col1):
+            if c not in grouped:
+                grouped[c] = work.tile([P, COLS, PACK], BF16, name="grouped", align_bytes=64)
+            engine_copy(
+                grouped[c][:, col0:col1, :].rearrange("p (c i) t -> p c t i", i=4),
+                w_raw[c][:, :, col0:col1].rearrange("p t (c i) -> p c t i", i=4),
+            )
+
+        def v_cols(c):
+            return V_COLS_HEAD if c <= PASSES else V_COLS
+
+        def interleave_v(c):
+            interleave(nc.vector.tensor_copy, c, 0, v_cols(c))
+
+        def interleave_s(c):
+            interleave(nc.scalar.copy, c, v_cols(c), COLS)
+
+        def quantize_w(c):
+            w_codes[c] = work.tile([P, COLS], U32, name="w_codes", bufs=6, align_bytes=64)
+            w_scales[c] = work.tile([P, COLS], U8, name="w_scales", bufs=6, align_bytes=64)
+            nc.vector.quantize_mx(
+                out=w_codes[c][:].bitcast(E5M2X4),
+                scales=w_scales[c][:],
+                in_=grouped[c][:].rearrange("p n t -> p (n t)"),
+            )
+
+        def transpose_x(tt):
+            words = x_raw[tt][:].bitcast(F32)
+            for half in range(2):
+                xb = bank(TOKEN_TILES + 2 * (tt % 2) + half)
+                x_banks[tt, half] = xb
+                for gl in range(2):
+                    g = 2 * half + gl
+                    for u in range(2):
+                        col = (2 * gl + u) * P
+                        nc.tensor.transpose(
+                            xb[:, col : col + P], words[:, 2 * P * g + u : 2 * P * (g + 1) : 2], ident[:]
+                        )
+
+        def copy_x(tt):
+            x_grouped[tt] = work.tile([P, M], BF16, name="x_grouped", bufs=2, align_bytes=64)
+            words = x_grouped[tt][:].bitcast(F32)
+            for half in range(2):
+                nc.scalar.copy(
+                    words[:, half * COLS : (half + 1) * COLS].rearrange("p (g r u) -> p g r u", g=2, u=2),
+                    x_banks[tt, half][:].rearrange("p (g u r) -> p g r u", g=2, u=2),
+                )
+
+        def quantize_x(tt):
+            x_codes[tt] = keep.tile([P, PASSES * P], U32, name="x_codes%d" % tt, align_bytes=64)
+            x_scales[tt] = keep.tile([P, PASSES * P], U8, name="x_scales%d" % tt, align_bytes=64)
+            nc.vector.quantize_mx(
+                out=x_codes[tt][:].bitcast(E5M2X4), scales=x_scales[tt][:], in_=x_grouped[tt][:]
+            )
+
+        def multiply(c, tt):
+            j, g = divmod(c, PASSES)
+            b = j * TOKEN_TILES + tt
+            if g == 0:
+                acc[b] = bank(TOKEN_TILES * (j % 2) + tt)
+            tokens = slice(g * P, (g + 1) * P)
+            nc.tensor.matmul_mx(
+                out=acc[b][:],
+                lhsT=x_codes[tt][:, tokens].bitcast(E5M2X4),
+                lhsT_scale=x_scales[tt][:, tokens],
+                rhs=w_codes[c][:].bitcast(E5M2X4),
+                rhs_scale=w_scales[c][:],
+                start=(g == 0),
+                stop=(g == PASSES - 1),
+            )
+
+        def squares(b):
+            sum_sq[b] = work.tile([P, HEADS], F32, name="sum_sq")
+            squared = work.tile([P, COLS], F32, name="squared", bufs=2)
+            for h in range(HEADS):
+                cols = slice(h * HD, (h + 1) * HD)
+                nc.scalar.activation(
+                    squared[:, cols], acc[b][:, cols], ACT.Square, accum_out=sum_sq[b][:, h : h + 1]
+                )
+
+        def root(b):
+            inv_rms[b] = work.tile([P, HEADS], F32, name="inv_rms")
+            nc.scalar.activation(inv_rms[b][:], sum_sq[b][:], ACT.Abs_reciprocal_sqrt, bias=EPS, scale=1.0 / HD)
+
+        def store(b, result):
+            j, tt = divmod(b, TOKEN_TILES)
+            nc.sync.dma_start(out=outs[j][tt * P : (tt + 1) * P, :], in_=result[:])
+
+        def normalise(b):
+            j, tt = divmod(b, TOKEN_TILES)
+            w = gain_of_tile[j]
+            pos = tt % POS_TILES
+            y = acc[b][:].rearrange("p (h d) -> p h d", h=HEADS)
+            result = keep.tile([P, COLS], F32, name="result%d" % b)
+            res = result[:].rearrange("p (h d) -> p h d", h=HEADS)
+            turned = work.tile([P, HEADS, ROT], F32, name="turned")
+            for h in range(HEADS):
+                nc.vector.scalar_tensor_tensor(
+                    res[:, h, :], y[:, h, :], inv_rms[b][:, h : h + 1], direct[:, w, pos, :], ALU.mult, ALU.mult
+                )
+            for h in range(HEADS):
+                nc.vector.scalar_tensor_tensor(
+                    turned[:, h, :], y[:, h, 0:ROT], inv_rms[b][:, h : h + 1], cross[:, w, pos, :], ALU.mult, ALU.mult
+                )
+            return result, turned
+
+        def finish(b, result, turned):
+            res = result[:].rearrange("p (h d) -> p h d", h=HEADS)
+            for lo, hi in ((0, HALF), (HALF, 0)):
+                nc.vector.tensor_tensor(
+                    res[:, :, lo : lo + HALF], res[:, :, lo : lo + HALF], turned[:, :, hi : hi + HALF], ALU.add
+                )
+            store(b, result)
+
+        interleave_v(0)
+        interleave_s(0)
+        transpose_x(0)
+        gains = bank(TOKEN_TILES - 1)
+        nc.tensor.matmul(gains[:, 0 : 2 * HD], lhsT=ones[:], rhs=gain_rows[:], start=True, stop=True)
+        for s in range(PASSES):
+            quantize_w(s)
+            if s == 1:
+                build_tables(gains)
+            copy_x(s)
+            interleave_v(s + 1)
+            interleave_s(s + 1)
+            quantize_x(s)
+            if s + 1 < TOKEN_TILES:
+                transpose_x(s + 1)
+            for tt in range(s):
+                multiply(s, tt)
+            for g in range(s + 1):
+                multiply(g, s)
+
+        pending = {}
+        for s in range(PASSES, CHUNKS):
+            b = s - PASSES
+            squares(b)
+            if s + 1 < CHUNKS:
+                interleave_v(s + 1)
+                interleave_s(s + 1)
+            root(b)
+            if b >= 2:
+                finish(b - 2, *pending[b - 2])
+            quantize_w(s)
+            if b >= 1:
+                pending[b - 1] = normalise(b - 1)
+            for tt in range(TOKEN_TILES):
+                multiply(s, tt)
+
+        def copy_out(engine_copy, b):
+            result = keep.tile([P, COLS], F32, name="result%d" % b)
+            engine_copy(result[:], acc[b][:])
+            store(b, result)
+
+        last = NORMED_BANKS - 1
+        pending[last] = normalise(last)
+        copy_out(nc.scalar.copy, last + 1)
+        copy_out(nc.scalar.copy, last + 2)
+        finish(last - 1, *pending[last - 1])
+        finish(last, *pending[last])
+        copy_out(nc.scalar.copy, last + 3)
+        copy_out(nc.vector.tensor_copy, last + 4)

@@ -31,8 +31,15 @@ HEADS = COLS // HD
 COL_TILES = (H + 2 * KV) // HEADS
 CHUNKS = COL_TILES * PASSES
 NORMED_BANKS = (COL_TILES - 1) * TOKEN_TILES
-V_COLS_HEAD = 328
+X_TILE_OF_STEP = {0: 0, 1: 1, 3: 2, 4: 3}
+TABLE_STEP = 2
+V_COLS_X = 344
+V_COLS_TABLES = 136
+V_COLS_X_SQUARES = 424
 V_COLS = 216
+V_COLS_SHARED = 144
+G_COLS = 112
+FIRST_G_CHUNK = PASSES + 3
 
 
 def tile_qwen3_5attention_pa_kernel(
@@ -67,9 +74,6 @@ def tile_qwen3_5attention_pa_kernel(
         ident = keep.tile([P, P], F32)
         make_identity(nc, ident[:])
 
-        nc.scalar.dma_start(out=gain_rows[0:1, 0:HD], in_=q_scale.rearrange("(o d) -> o d", o=1))
-        nc.scalar.dma_start(out=gain_rows[0:1, HD : 2 * HD], in_=k_scale.rearrange("(o d) -> o d", o=1))
-
         w_raw = []
         x_raw = []
 
@@ -79,14 +83,20 @@ def tile_qwen3_5attention_pa_kernel(
             nc.sync.dma_start(out=raw[:], in_=rows.rearrange("(p t) n -> p t n", t=PACK))
             return raw
 
-        for g in range(PASSES):
-            w_raw.append(load_w(wk, 0, COLS, g)[:])
-            xt = keep.tile([P, M], BF16, name="x_raw%d" % g, align_bytes=64)
-            nc.sync.dma_start(out=xt[:], in_=x_hbm[g * P : (g + 1) * P, :])
-            x_raw.append(xt)
-        for col0 in (0, COLS):
-            for g in range(PASSES):
-                w_raw.append(load_w(wq, col0, COLS, g)[:])
+        def load_x(tt):
+            raw = keep.tile([P, M], BF16, name="x_raw%d" % tt, align_bytes=64)
+            nc.sync.dma_start(out=raw[:], in_=x_hbm[tt * P : (tt + 1) * P, :])
+            x_raw.append(raw)
+
+        narrow = [(wk, 0), (wq, 0), (wq, COLS)]
+        for c in range(len(narrow) * PASSES):
+            w, col0 = narrow[c // PASSES]
+            w_raw.append(load_w(w, col0, COLS, c % PASSES)[:])
+            if c in X_TILE_OF_STEP:
+                load_x(X_TILE_OF_STEP[c])
+            if c == 0:
+                nc.sync.dma_start(out=gain_rows[0:1, 0:HD], in_=q_scale.rearrange("(o d) -> o d", o=1))
+                nc.sync.dma_start(out=gain_rows[0:1, HD : 2 * HD], in_=k_scale.rearrange("(o d) -> o d", o=1))
         wide = []
         for g in range(PASSES):
             raw = load_w(wq, 2 * COLS, 2 * COLS, g)
@@ -134,7 +144,7 @@ def tile_qwen3_5attention_pa_kernel(
             nc.vector.tensor_tensor(cross[:, :, :, 0:HALF], lo, sin, ALU.mult)
             nc.vector.tensor_tensor(cross[:, :, :, HALF:ROT], hi, neg_sin[:].to_broadcast(shape), ALU.mult)
 
-        grouped = {}
+        grouped = keep.tile([P, 2, COLS, PACK], BF16, align_bytes=64)
         w_codes = {}
         w_scales = {}
         x_banks = {}
@@ -144,37 +154,51 @@ def tile_qwen3_5attention_pa_kernel(
         acc = {}
         sum_sq = {}
         inv_rms = {}
+        turned = {}
+        results = {}
 
         def interleave(engine_copy, c, col0, col1):
-            if c not in grouped:
-                grouped[c] = work.tile([P, COLS, PACK], BF16, name="grouped", align_bytes=64)
             engine_copy(
-                grouped[c][:, col0:col1, :].rearrange("p (c i) t -> p c t i", i=4),
+                grouped[:, c % 2, col0:col1, :].rearrange("p (c i) t -> p c t i", i=4),
                 w_raw[c][:, :, col0:col1].rearrange("p t (c i) -> p c t i", i=4),
             )
 
-        def v_cols(c):
-            return V_COLS_HEAD if c <= PASSES else V_COLS
+        def v_range(c):
+            step = max(c - 1, 0)
+            if step in X_TILE_OF_STEP:
+                return 0, V_COLS_X if step < PASSES else V_COLS_X_SQUARES
+            if step == TABLE_STEP:
+                return 0, V_COLS_TABLES
+            if c < FIRST_G_CHUNK:
+                return 0, V_COLS
+            return G_COLS, G_COLS + V_COLS_SHARED
 
         def interleave_v(c):
-            interleave(nc.vector.tensor_copy, c, 0, v_cols(c))
+            interleave(nc.vector.tensor_copy, c, *v_range(c))
 
         def interleave_s(c):
-            interleave(nc.scalar.copy, c, v_cols(c), COLS)
+            interleave(nc.scalar.copy, c, v_range(c)[1], COLS)
 
-        def quantize_w(c):
+        def interleave_g(c):
+            nc.gpsimd.tensor_copy(
+                grouped[:, c % 2, 0:G_COLS, :], w_raw[c][:, :, 0:G_COLS].rearrange("p t n -> p n t")
+            )
+
+        def quantize_w(c, pieces):
             w_codes[c] = work.tile([P, COLS], U32, name="w_codes", bufs=6, align_bytes=64)
             w_scales[c] = work.tile([P, COLS], U8, name="w_scales", bufs=6, align_bytes=64)
-            nc.vector.quantize_mx(
-                out=w_codes[c][:].bitcast(E5M2X4),
-                scales=w_scales[c][:],
-                in_=grouped[c][:].rearrange("p n t -> p (n t)"),
-            )
+            for col in range(0, COLS, COLS // pieces):
+                cols = slice(col, col + COLS // pieces)
+                nc.vector.quantize_mx(
+                    out=w_codes[c][:, cols].bitcast(E5M2X4),
+                    scales=w_scales[c][:, cols],
+                    in_=grouped[:, c % 2, cols, :].rearrange("p n t -> p (n t)"),
+                )
 
         def transpose_x(tt):
             words = x_raw[tt][:].bitcast(F32)
             for half in range(2):
-                xb = bank(TOKEN_TILES + 2 * (tt % 2) + half)
+                xb = bank(tt + TOKEN_TILES * half)
                 x_banks[tt, half] = xb
                 for gl in range(2):
                     g = 2 * half + gl
@@ -233,54 +257,71 @@ def tile_qwen3_5attention_pa_kernel(
             j, tt = divmod(b, TOKEN_TILES)
             nc.sync.dma_start(out=outs[j][tt * P : (tt + 1) * P, :], in_=result[:])
 
-        def normalise(b):
+        def table_row(b):
             j, tt = divmod(b, TOKEN_TILES)
-            w = gain_of_tile[j]
-            pos = tt % POS_TILES
+            return gain_of_tile[j], tt % POS_TILES
+
+        def normalise(b):
+            w, pos = table_row(b)
             y = acc[b][:].rearrange("p (h d) -> p h d", h=HEADS)
-            result = keep.tile([P, COLS], F32, name="result%d" % b)
-            res = result[:].rearrange("p (h d) -> p h d", h=HEADS)
-            turned = work.tile([P, HEADS, ROT], F32, name="turned")
+            results[b] = keep.tile([P, COLS], F32, name="result%d" % b)
+            res = results[b][:].rearrange("p (h d) -> p h d", h=HEADS)
+            turned[b] = work.tile([P, HEADS, ROT], F32, name="turned")
             for h in range(HEADS):
                 nc.vector.scalar_tensor_tensor(
                     res[:, h, :], y[:, h, :], inv_rms[b][:, h : h + 1], direct[:, w, pos, :], ALU.mult, ALU.mult
                 )
             for h in range(HEADS):
                 nc.vector.scalar_tensor_tensor(
-                    turned[:, h, :], y[:, h, 0:ROT], inv_rms[b][:, h : h + 1], cross[:, w, pos, :], ALU.mult, ALU.mult
+                    turned[b][:, h, :], y[:, h, 0:ROT], inv_rms[b][:, h : h + 1], cross[:, w, pos, :], ALU.mult, ALU.mult
                 )
-            return result, turned
 
-        def finish(b, result, turned):
-            res = result[:].rearrange("p (h d) -> p h d", h=HEADS)
-            for lo, hi in ((0, HALF), (HALF, 0)):
-                nc.vector.tensor_tensor(
-                    res[:, :, lo : lo + HALF], res[:, :, lo : lo + HALF], turned[:, :, hi : hi + HALF], ALU.add
-                )
-            store(b, result)
+        def finish(b):
+            res = results[b][:].rearrange("p (h d) -> p h d", h=HEADS)
+            rotary = res[:, :, 0:ROT].rearrange("p h (u i) -> p h u i", u=2)
+            swapped = turned[b][:].rearrange("p h (u i) -> p h u i", u=2)[:, :, ::-1, :]
+            nc.vector.tensor_tensor(rotary, rotary, swapped, ALU.add)
+            store(b, results[b])
+
+        def multiply_step(s):
+            next_tile = X_TILE_OF_STEP.get(s + 1)
+            closes_banks = s % PASSES == PASSES - 1
+            if next_tile is not None and not closes_banks:
+                transpose_x(next_tile)
+            new_tile = X_TILE_OF_STEP.get(s)
+            for tt in x_codes:
+                if tt != new_tile:
+                    multiply(s, tt)
+            if next_tile is not None and closes_banks:
+                transpose_x(next_tile)
+            if new_tile is not None:
+                for c in range(s + 1):
+                    multiply(c, new_tile)
 
         interleave_v(0)
         interleave_s(0)
         transpose_x(0)
-        gains = bank(TOKEN_TILES - 1)
+        gains = bank(2 * TOKEN_TILES - 1)
         nc.tensor.matmul(gains[:, 0 : 2 * HD], lhsT=ones[:], rhs=gain_rows[:], start=True, stop=True)
-        for s in range(PASSES):
-            quantize_w(s)
-            if s == 1:
+
+        for s in range(max(X_TILE_OF_STEP) + 1):
+            b = s - PASSES
+            if b >= 0:
+                squares(b)
+            quantize_w(s, 1)
+            if s == TABLE_STEP:
                 build_tables(gains)
-            copy_x(s)
+            if s in X_TILE_OF_STEP:
+                copy_x(X_TILE_OF_STEP[s])
             interleave_v(s + 1)
             interleave_s(s + 1)
-            quantize_x(s)
-            if s + 1 < TOKEN_TILES:
-                transpose_x(s + 1)
-            for tt in range(s):
-                multiply(s, tt)
-            for g in range(s + 1):
-                multiply(g, s)
+            if s in X_TILE_OF_STEP:
+                quantize_x(X_TILE_OF_STEP[s])
+            if b >= 0:
+                root(b)
+            multiply_step(s)
 
-        pending = {}
-        for s in range(PASSES, CHUNKS):
+        for s in range(max(X_TILE_OF_STEP) + 1, CHUNKS):
             b = s - PASSES
             squares(b)
             if s + 1 < CHUNKS:
@@ -288,12 +329,14 @@ def tile_qwen3_5attention_pa_kernel(
                 interleave_s(s + 1)
             root(b)
             if b >= 2:
-                finish(b - 2, *pending[b - 2])
-            quantize_w(s)
-            if b >= 1:
-                pending[b - 1] = normalise(b - 1)
-            for tt in range(TOKEN_TILES):
-                multiply(s, tt)
+                finish(b - 2)
+            if s + 2 < CHUNKS:
+                quantize_w(s, 2)
+                interleave_g(s + 2)
+            else:
+                quantize_w(s, 1)
+            normalise(b - 1)
+            multiply_step(s)
 
         def copy_out(engine_copy, b):
             result = keep.tile([P, COLS], F32, name="result%d" % b)
@@ -301,10 +344,10 @@ def tile_qwen3_5attention_pa_kernel(
             store(b, result)
 
         last = NORMED_BANKS - 1
-        pending[last] = normalise(last)
+        normalise(last)
+        finish(last - 1)
         copy_out(nc.scalar.copy, last + 1)
         copy_out(nc.scalar.copy, last + 2)
-        finish(last - 1, *pending[last - 1])
-        finish(last, *pending[last])
+        finish(last)
         copy_out(nc.scalar.copy, last + 3)
         copy_out(nc.vector.tensor_copy, last + 4)

@@ -123,6 +123,8 @@ def tile_qwen3_5attention_pa_kernel(
         nc.scalar.activation(
             trig[:].rearrange("p f o h i -> p (f o h i)"), neg_frac[:], ACT.Sin, scale=-2.0 * math.pi
         )
+        warm = keep.tile([P, 1], F32)
+        nc.scalar.activation(warm[:], ones[:, 0:1], ACT.Abs_reciprocal_sqrt, bias=EPS, scale=1.0 / HD)
 
         direct = keep.tile([P, 2, POS_TILES, HD], F32)
         cross = keep.tile([P, 2, POS_TILES, ROT], F32)

import math
from contextlib import ExitStack

import concourse.mybir as mybir
from concourse.masks import make_identity

B, S, M, H, KV, HD = 2, 256, 2048, 16, 4, 128
ROT = HD // 4
HALF = ROT // 2
EPS = 1e-6
MAX_WAVELENGTH = 10000.0
FLOPS = 2 * B * S * M * (H + 2 * KV) * HD

F32 = mybir.dt.float32
BF16 = mybir.dt.bfloat16
I32 = mybir.dt.int32
U32 = mybir.dt.uint32
U8 = mybir.dt.uint8
E5M2X4 = mybir.dt.float8_e5m2_x4
ALU = mybir.AluOpType
ACT = mybir.ActivationFunctionType

P = 128
PACK = 4
K_PASS = P * PACK
PASSES = M // K_PASS
TOKEN_TILES = B * S // P
POS_TILES = S // P
COLS = 512
HEADS = COLS // HD
COL_TILES = (H + 2 * KV) // HEADS
CHUNKS = COL_TILES * PASSES
NORMED_BANKS = (COL_TILES - 1) * TOKEN_TILES
X_TILE_OF_STEP = {0: 0, 1: 1, 3: 2, 4: 3}
TABLE_STEP = 2
V_COLS_X = 344
V_COLS_TABLES = 136
V_COLS_X_SQUARES = 424
V_COLS = 216
V_COLS_SHARED = 144
G_COLS = 112
FIRST_G_CHUNK = PASSES + 3


def tile_qwen3_5attention_pa_kernel(
    tc, hidden_states, Wq_query, Wk, Wv, q_scale, k_scale, out_0, out_1, out_2
):
    nc = tc.nc
    x_hbm = hidden_states.rearrange("b s m -> (b s) m")
    wq = Wq_query.rearrange("m h d -> m (h d)")
    wk = Wk.rearrange("m h d -> m (h d)")
    wv = Wv.rearrange("m h d -> m (h d)")
    q_out = out_0.rearrange("b s h d -> (b s) (h d)")
    k_out = out_1.rearrange("b s h d -> (b s) (h d)")
    v_out = out_2.rearrange("b s h d -> (b s) (h d)")
    outs = [k_out] + [q_out[:, c : c + COLS] for c in range(0, H * HD, COLS)] + [v_out]
    gain_of_tile = [1, 0, 0, 0, 0]

    with ExitStack() as ctx:
        keep = ctx.enter_context(tc.tile_pool(name="keep", bufs=1))
        work = ctx.enter_context(tc.tile_pool(name="work", bufs=3))
        psum = ctx.enter_context(tc.psum_pool(name="psum", bufs=1))
        ctx.enter_context(tc.manual_schedule())

        def bank(index):
            return psum.tile([P, COLS], F32, name="bank%d" % index)

        gain_rows = keep.tile([P, 2 * HD], BF16)
        nc.gpsimd.memset(gain_rows[:], 0.0)
        position = keep.tile([P, POS_TILES], I32)
        nc.gpsimd.iota(position[:], pattern=[[P, POS_TILES]], base=0, channel_multiplier=1)
        ones = keep.tile([P, P], BF16)
        nc.gpsimd.memset(ones[:], 1.0)
        ident = keep.tile([P, P], F32)
        make_identity(nc, ident[:])

        w_raw = []
        x_raw = []

        def load_w(w, col0, width, g):
            raw = keep.tile([P, PACK, width], BF16, name="w_raw%d" % len(w_raw), align_bytes=64)
            rows = w[g * K_PASS : (g + 1) * K_PASS, col0 : col0 + width]
            nc.sync.dma_start(out=raw[:], in_=rows.rearrange("(p t) n -> p t n", t=PACK))
            return raw

        def load_x(tt):
            raw = keep.tile([P, M], BF16, name="x_raw%d" % tt, align_bytes=64)
            nc.sync.dma_start(out=raw[:], in_=x_hbm[tt * P : (tt + 1) * P, :])
            x_raw.append(raw)

        narrow = [(wk, 0), (wq, 0), (wq, COLS)]
        for c in range(len(narrow) * PASSES):
            w, col0 = narrow[c // PASSES]
            w_raw.append(load_w(w, col0, COLS, c % PASSES)[:])
            if c in X_TILE_OF_STEP:
                load_x(X_TILE_OF_STEP[c])
            if c == 0:
                nc.sync.dma_start(out=gain_rows[0:1, 0:HD], in_=q_scale.rearrange("(o d) -> o d", o=1))
                nc.sync.dma_start(out=gain_rows[0:1, HD : 2 * HD], in_=k_scale.rearrange("(o d) -> o d", o=1))
        wide = []
        for g in range(PASSES):
            raw = load_w(wq, 2 * COLS, 2 * COLS, g)
            wide.append(raw)
            w_raw.append(raw[:, :, 0:COLS])
        for g in range(PASSES):
            w_raw.append(wide[g][:, :, COLS : 2 * COLS])
        for g in range(PASSES):
            w_raw.append(load_w(wv, 0, COLS, g)[:])

        turns = keep.tile([P, 2, POS_TILES, HALF], F32)
        for i in range(HALF):
            per_position = MAX_WAVELENGTH ** (-i / HALF) / (2.0 * math.pi)
            nc.vector.tensor_scalar(turns[:, 1, :, i], position[:], per_position, None, ALU.mult)
        nc.vector.tensor_scalar(turns[:, 0, :, :], turns[:, 1, :, :], 0.25, None, ALU.add)
        flat_turns = turns[:].rearrange("p f h i -> p (f h i)")
        whole = keep.tile([P, 2 * POS_TILES * HALF], I32)
        nc.vector.tensor_copy(whole[:], flat_turns)
        frac = keep.tile([P, 2 * POS_TILES * HALF], F32)
        nc.vector.tensor_tensor(frac[:], flat_turns, whole[:], ALU.subtract)
        neg_frac = keep.tile([P, 2 * POS_TILES * HALF], F32)
        nc.vector.scalar_tensor_tensor(neg_frac[:], frac[:], 0.5, frac[:], ALU.is_gt, ALU.subtract)
        trig = keep.tile([P, 2, 1, POS_TILES, HALF], F32)
        nc.scalar.activation(
            trig[:].rearrange("p f o h i -> p (f o h i)"), neg_frac[:], ACT.Sin, scale=-2.0 * math.pi
        )
        warm = keep.tile([P, 1], F32)
        nc.scalar.activation(warm[:], ones[:, 0:1], ACT.Abs_reciprocal_sqrt, bias=EPS, scale=1.0 / HD)

        direct = keep.tile([P, 2, POS_TILES, HD], F32)
        cross = keep.tile([P, 2, POS_TILES, ROT], F32)

        def build_tables(gains):
            g4 = gains[:, 0 : 2 * HD].rearrange("p (w o d) -> p w o d", w=2, o=1)
            shape = [P, 2, POS_TILES, HALF]
            cos = trig[:, 0, :, :, :].to_broadcast(shape)
            sin = trig[:, 1, :, :, :].to_broadcast(shape)
            neg_sin = keep.tile([P, 1, POS_TILES, HALF], F32)
            nc.vector.tensor_scalar(neg_sin[:], trig[:, 1, :, :, :], -1.0, None, ALU.mult)
            lo = g4[:, :, :, 0:HALF].to_broadcast(shape)
            hi = g4[:, :, :, HALF:ROT].to_broadcast(shape)
            nc.vector.tensor_tensor(direct[:, :, :, 0:HALF], lo, cos, ALU.mult)
            nc.vector.tensor_tensor(direct[:, :, :, HALF:ROT], hi, cos, ALU.mult)
            nc.vector.tensor_copy(
                direct[:, :, :, ROT:HD], g4[:, :, :, ROT:HD].to_broadcast([P, 2, POS_TILES, HD - ROT])
            )
            nc.vector.tensor_tensor(cross[:, :, :, 0:HALF], lo, sin, ALU.mult)
            nc.vector.tensor_tensor(cross[:, :, :, HALF:ROT], hi, neg_sin[:].to_broadcast(shape), ALU.mult)

        grouped = keep.tile([P, 2, COLS, PACK], BF16, align_bytes=64)
        w_codes = {}
        w_scales = {}
        x_banks = {}
        x_grouped = {}
        x_codes = {}
        x_scales = {}
        acc = {}
        sum_sq = {}
        inv_rms = {}
        turned = {}
        results = {}

        def interleave(engine_copy, c, col0, col1):
            engine_copy(
                grouped[:, c % 2, col0:col1, :].rearrange("p (c i) t -> p c t i", i=4),
                w_raw[c][:, :, col0:col1].rearrange("p t (c i) -> p c t i", i=4),
            )

        def v_range(c):
            step = max(c - 1, 0)
            if step in X_TILE_OF_STEP:
                return 0, V_COLS_X if step < PASSES else V_COLS_X_SQUARES
            if step == TABLE_STEP:
                return 0, V_COLS_TABLES
            if c < FIRST_G_CHUNK:
                return 0, V_COLS
            return G_COLS, G_COLS + V_COLS_SHARED

        def interleave_v(c):
            interleave(nc.vector.tensor_copy, c, *v_range(c))

        def interleave_s(c):
            interleave(nc.scalar.copy, c, v_range(c)[1], COLS)

        def interleave_g(c):
            nc.gpsimd.tensor_copy(
                grouped[:, c % 2, 0:G_COLS, :], w_raw[c][:, :, 0:G_COLS].rearrange("p t n -> p n t")
            )

        def quantize_w(c, pieces):
            w_codes[c] = work.tile([P, COLS], U32, name="w_codes", bufs=6, align_bytes=64)
            w_scales[c] = work.tile([P, COLS], U8, name="w_scales", bufs=6, align_bytes=64)
            for col in range(0, COLS, COLS // pieces):
                cols = slice(col, col + COLS // pieces)
                nc.vector.quantize_mx(
                    out=w_codes[c][:, cols].bitcast(E5M2X4),
                    scales=w_scales[c][:, cols],
                    in_=grouped[:, c % 2, cols, :].rearrange("p n t -> p (n t)"),
                )

        def transpose_x(tt):
            words = x_raw[tt][:].bitcast(F32)
            for half in range(2):
                xb = bank(tt + TOKEN_TILES * half)
                x_banks[tt, half] = xb
                for gl in range(2):
                    g = 2 * half + gl
                    for u in range(2):
                        col = (2 * gl + u) * P
                        nc.tensor.transpose(
                            xb[:, col : col + P], words[:, 2 * P * g + u : 2 * P * (g + 1) : 2], ident[:]
                        )

        def copy_x(tt):
            x_grouped[tt] = work.tile([P, M], BF16, name="x_grouped", bufs=2, align_bytes=64)
            words = x_grouped[tt][:].bitcast(F32)
            for half in range(2):
                nc.scalar.copy(
                    words[:, half * COLS : (half + 1) * COLS].rearrange("p (g r u) -> p g r u", g=2, u=2),
                    x_banks[tt, half][:].rearrange("p (g u r) -> p g r u", g=2, u=2),
                )

        def quantize_x(tt):
            x_codes[tt] = keep.tile([P, PASSES * P], U32, name="x_codes%d" % tt, align_bytes=64)
            x_scales[tt] = keep.tile([P, PASSES * P], U8, name="x_scales%d" % tt, align_bytes=64)
            nc.vector.quantize_mx(
                out=x_codes[tt][:].bitcast(E5M2X4), scales=x_scales[tt][:], in_=x_grouped[tt][:]
            )

        def multiply(c, tt):
            j, g = divmod(c, PASSES)
            b = j * TOKEN_TILES + tt
            if g == 0:
                acc[b] = bank(TOKEN_TILES * (j % 2) + tt)
            tokens = slice(g * P, (g + 1) * P)
            nc.tensor.matmul_mx(
                out=acc[b][:],
                lhsT=x_codes[tt][:, tokens].bitcast(E5M2X4),
                lhsT_scale=x_scales[tt][:, tokens],
                rhs=w_codes[c][:].bitcast(E5M2X4),
                rhs_scale=w_scales[c][:],
                start=(g == 0),
                stop=(g == PASSES - 1),
            )

        def squares(b):
            sum_sq[b] = work.tile([P, HEADS], F32, name="sum_sq")
            squared = work.tile([P, COLS], F32, name="squared", bufs=2)
            for h in range(HEADS):
                cols = slice(h * HD, (h + 1) * HD)
                nc.scalar.activation(
                    squared[:, cols], acc[b][:, cols], ACT.Square, accum_out=sum_sq[b][:, h : h + 1]
                )

        def root(b):
            inv_rms[b] = work.tile([P, HEADS], F32, name="inv_rms")
            nc.scalar.activation(inv_rms[b][:], sum_sq[b][:], ACT.Abs_reciprocal_sqrt, bias=EPS, scale=1.0 / HD)

        def store(b, result):
            j, tt = divmod(b, TOKEN_TILES)
            nc.sync.dma_start(out=outs[j][tt * P : (tt + 1) * P, :], in_=result[:])

        def table_row(b):
            j, tt = divmod(b, TOKEN_TILES)
            return gain_of_tile[j], tt % POS_TILES

        def normalise(b):
            w, pos = table_row(b)
            y = acc[b][:].rearrange("p (h d) -> p h d", h=HEADS)
            results[b] = keep.tile([P, COLS], F32, name="result%d" % b)
            res = results[b][:].rearrange("p (h d) -> p h d", h=HEADS)
            turned[b] = work.tile([P, HEADS, ROT], F32, name="turned")
            for h in range(HEADS):
                nc.vector.scalar_tensor_tensor(
                    res[:, h, :], y[:, h, :], inv_rms[b][:, h : h + 1], direct[:, w, pos, :], ALU.mult, ALU.mult
                )
            for h in range(HEADS):
                nc.vector.scalar_tensor_tensor(
                    turned[b][:, h, :], y[:, h, 0:ROT], inv_rms[b][:, h : h + 1], cross[:, w, pos, :], ALU.mult, ALU.mult
                )

        def finish(b):
            res = results[b][:].rearrange("p (h d) -> p h d", h=HEADS)
            rotary = res[:, :, 0:ROT].rearrange("p h (u i) -> p h u i", u=2)
            swapped = turned[b][:].rearrange("p h (u i) -> p h u i", u=2)[:, :, ::-1, :]
            nc.vector.tensor_tensor(rotary, rotary, swapped, ALU.add)
            store(b, results[b])

        def multiply_step(s):
            next_tile = X_TILE_OF_STEP.get(s + 1)
            closes_banks = s % PASSES == PASSES - 1
            if next_tile is not None and not closes_banks:
                transpose_x(next_tile)
            new_tile = X_TILE_OF_STEP.get(s)
            for tt in x_codes:
                if tt != new_tile:
                    multiply(s, tt)
            if next_tile is not None and closes_banks:
                transpose_x(next_tile)
            if new_tile is not None:
                for c in range(s + 1):
                    multiply(c, new_tile)

        interleave_v(0)
        interleave_s(0)
        transpose_x(0)
        gains = bank(2 * TOKEN_TILES - 1)
        nc.tensor.matmul(gains[:, 0 : 2 * HD], lhsT=ones[:], rhs=gain_rows[:], start=True, stop=True)

        for s in range(max(X_TILE_OF_STEP) + 1):
            b = s - PASSES
            if b >= 0:
                squares(b)
            quantize_w(s, 1)
            if s == TABLE_STEP:
                build_tables(gains)
            if s in X_TILE_OF_STEP:
                copy_x(X_TILE_OF_STEP[s])
            interleave_v(s + 1)
            interleave_s(s + 1)
            if s in X_TILE_OF_STEP:
                quantize_x(X_TILE_OF_STEP[s])
            if b >= 0:
                root(b)
            multiply_step(s)

        for s in range(max(X_TILE_OF_STEP) + 1, CHUNKS):
            b = s - PASSES
            squares(b)
            if s + 1 < CHUNKS:
                interleave_v(s + 1)
                interleave_s(s + 1)
            root(b)
            if b >= 2:
                finish(b - 2)
            if s + 2 < CHUNKS:
                quantize_w(s, 2)
                interleave_g(s + 2)
            else:
                quantize_w(s, 1)
            normalise(b - 1)
            multiply_step(s)

        def copy_out(engine_copy, b):
            result = keep.tile([P, COLS], F32, name="result%d" % b)
            engine_copy(result[:], acc[b][:])
            store(b, result)

        last = NORMED_BANKS - 1
        normalise(last)
        finish(last - 1)
        copy_out(nc.scalar.copy, last + 1)
        copy_out(nc.scalar.copy, last + 2)
        finish(last)
        copy_out(nc.scalar.copy, last + 3)
        copy_out(nc.vector.tensor_copy, last + 4)
